import numpy as np
import ml_dtypes


def mxq(x, axis, fmt="e4m3"):
    dtype, down = {"e4m3": (ml_dtypes.float8_e4m3fn, 7), "e5m2": (ml_dtypes.float8_e5m2, 14)}[fmt]
    v = np.moveaxis(np.asarray(x, np.float32).astype(ml_dtypes.bfloat16).astype(np.float64), axis, -1)
    blocks = v.reshape(v.shape[:-1] + (-1, 32))
    amax = np.abs(blocks).max(-1, keepdims=True)
    byte = np.maximum(np.where(amax > 0, np.frexp(amax)[1] - 1 + 127, 0) - down, 1)
    scale = np.exp2(byte - 127.0)
    codes = (blocks / scale).astype(np.float32).astype(dtype).astype(np.float64)
    return np.moveaxis((codes * scale).reshape(v.shape), -1, axis)


WIDE = False


def mx_kscale(k):
    if not WIDE:
        return np.ones(k)
    levels = np.array([10, -10, 5, -5, 0])
    a = np.random.permutation(np.resize(levels, k // 512 * 4)).reshape(k // 512, 4)
    idx = np.arange(k)
    return np.exp2(a[idx // 512, idx % 128 // 32])


BF16 = ml_dtypes.bfloat16


def bf(x):
    return np.asarray(x, np.float32).astype(BF16)


def f64(x):
    return np.asarray(x).astype(np.float64)


E2M1 = np.array([0.0, 0.5, 1.0, 1.5, 2.0, 3.0, 4.0, 6.0, -0.0, -0.5, -1.0, -1.5, -2.0, -3.0, -4.0, -6.0])


def pack_weight(w, fmt):
    k, n = w.shape
    w = f64(bf(w)).reshape(k // 32, 32, n)
    amax = np.abs(w).max(1)
    if fmt == "e4m3":
        byte = np.frexp(amax)[1] - 1 + 127 - 7
    else:
        mant, ex = np.frexp(amax / 6.0)
        byte = np.where(mant > 0.5, ex, ex - 1) + 127
    byte = np.clip(np.where(amax > 0, byte, 1), 1, 254)
    scaled = (w * np.exp2(127.0 - byte)[:, None, :]).reshape(k, n).astype(np.float32)
    by_word = np.ascontiguousarray(scaled.reshape(k // 512, 128, 4, n).transpose(0, 1, 3, 2))
    if fmt == "e4m3":
        words = by_word.astype(ml_dtypes.float8_e4m3fn).view(np.uint8)
    else:
        c = by_word.astype(ml_dtypes.float4_e2m1fn).view(np.uint8) & 0xF
        words = c[..., 0::2] | (c[..., 1::2] << 4)
    return np.ascontiguousarray(words), np.ascontiguousarray(byte.astype(np.uint8).reshape(k // 512, 16, n))


def unpack_weight(words, scales, fmt):
    g, p, n, _ = words.shape
    if fmt == "e4m3":
        vals = np.ascontiguousarray(words).view(ml_dtypes.float8_e4m3fn).astype(np.float64)
    else:
        nib = np.empty((g, p, n, 4), np.uint8)
        nib[..., 0::2] = words & 0xF
        nib[..., 1::2] = words >> 4
        vals = E2M1[nib]
    vals = vals * np.repeat(np.exp2(scales.astype(np.float64) - 127.0), 8, axis=1)[..., None]
    return vals.transpose(0, 1, 3, 2).reshape(g * 512, n)


B, N, DM, H = 2, 64, 2560, 20
LN_EPS = 1e-5
ROPE_BASE = 10000.0
FMT = "e4m3"


def rotate_half(x):
    d2 = x.shape[-1] // 2
    x1, x2 = x[..., :d2], x[..., d2:]
    return np.concatenate((-x2, x1), axis=-1)


def rotary_pos_emb(n, head_dim):
    inv_freq = 1.0 / (ROPE_BASE ** (np.arange(0.0, head_dim, 2.0) / head_dim))
    t = np.arange(0.0, n, 1.0)
    freqs = t[:, None] * inv_freq[None, :]
    return np.concatenate((freqs, freqs), axis=-1)


def apply_rotary(pos, t):
    return t * np.cos(pos) + rotate_half(t) * np.sin(pos)


def setup_inputs():
    s = mx_kscale(DM)
    r = np.exp2(np.random.uniform(-9.0, 1.0, (B, N, 1)))
    x = bf((np.random.standard_normal((B, N, DM)) + 0.5) * r)
    ln_gamma = bf((1.0 + 0.1 * np.random.standard_normal(DM)) * s)
    ln_beta = bf(0.1 * np.random.standard_normal(DM) * s)
    wq = np.random.standard_normal((DM, DM)) / np.sqrt(DM) / s[None, :]
    wk = np.random.standard_normal((DM, DM)) / np.sqrt(DM) / s[None, :]
    wv = np.random.standard_normal((DM, DM)) / np.sqrt(DM) / s[None, :]
    wq_words, wq_scales = pack_weight(np.ascontiguousarray(wq.T), FMT)
    wk_words, wk_scales = pack_weight(np.ascontiguousarray(wk.T), FMT)
    wv_words, wv_scales = pack_weight(np.ascontiguousarray(wv.T), FMT)
    return {"x": x,
            "ln_gamma": ln_gamma,
            "ln_beta": ln_beta,
            "wq_words": wq_words, "wq_scales": wq_scales,
            "wk_words": wk_words, "wk_scales": wk_scales,
            "wv_words": wv_words, "wv_scales": wv_scales,
            "num_heads": H}


def reference(x, ln_gamma, ln_beta, wq_words, wq_scales, wk_words, wk_scales, wv_words, wv_scales, num_heads):
    x = f64(x)
    b, n, dm = x.shape
    hd = dm // num_heads
    mu = np.mean(x, axis=-1, keepdims=True)
    var = np.mean(np.square(x - mu), axis=-1, keepdims=True)
    xn = (x - mu) / np.sqrt(var + LN_EPS) * f64(ln_gamma) + f64(ln_beta)
    xq = mxq(xn, 2, "e4m3")
    q = xq @ unpack_weight(wq_words, wq_scales, FMT)
    k = xq @ unpack_weight(wk_words, wk_scales, FMT)
    v = xq @ unpack_weight(wv_words, wv_scales, FMT)
    split = lambda t: t.reshape(b, n, num_heads, hd).transpose(0, 2, 1, 3)
    q, k, v = split(q), split(k), split(v)
    pos = rotary_pos_emb(n, hd)
    q = apply_rotary(pos, q)
    k = apply_rotary(pos, k)
    return q, k, v

@@ -1,0 +1,254 @@
+import math
+from contextlib import ExitStack
+
+import concourse.mybir as mybir
+from concourse.masks import make_identity
+
+F32 = mybir.dt.float32
+BF16 = mybir.dt.bfloat16
+I32 = mybir.dt.int32
+U32 = mybir.dt.uint32
+U8 = mybir.dt.uint8
+FP8X4 = mybir.dt.float8_e4m3fn_x4
+ALU = mybir.AluOpType
+ACT = mybir.ActivationFunctionType
+
+P = 128
+B, T, DM = 2, 64, 2560
+PACK = 4
+K_PASS = P * PACK
+G = DM // K_PASS
+HEAD = 128
+HALF = HEAD // 2
+BANK = 512
+HEADS_PER_BANK = BANK // HEAD
+LN_EPS = 1e-5
+ROPE_BASE = 10000.0
+
+QUADRANTS = 4
+PLANE_ROWS = 4
+PLANES_PER_SLOT = 4
+LAST_GROUP_SLOT = 3
+
+TURN_HI = 6.28125
+TURN_LO = 2.0 * math.pi - TURN_HI
+
+COLUMN_PARTS = (((0, DM),), ((0, DM),), ((0, DM - BANK), (DM - BANK, DM)))
+
+FLOPS = 2 * P * DM * 3 * DM
+
+
+def scale_plane(planes, weight, g, columns):
+    if g < PLANES_PER_SLOT:
+        first_row, slot = PLANE_ROWS * g, weight
+    else:
+        first_row, slot = PLANE_ROWS * weight, LAST_GROUP_SLOT
+    return planes[first_row:P, slot, columns]
+
+
+def load_scale_planes(nc, planes, all_scales):
+    nc.vector.memset(planes[:].bitcast(I32), 0)
+    for quadrant in range(QUADRANTS):
+        rows = slice(PLANE_ROWS * quadrant, PLANE_ROWS * (quadrant + 1))
+        first = 32 * quadrant
+        for weight, scales in enumerate(all_scales):
+            nc.sync.dma_start(
+                out=planes[first : first + PLANES_PER_SLOT * PLANE_ROWS, weight, :].bitcast(I32),
+                in_=scales[0:PLANES_PER_SLOT, rows, :].bitcast(I32),
+            )
+            mine = first + PLANE_ROWS * weight
+            nc.sync.dma_start(
+                out=planes[mine : mine + PLANE_ROWS, LAST_GROUP_SLOT, :].bitcast(I32),
+                in_=scales[PLANES_PER_SLOT, rows, :].bitcast(I32),
+            )
+
+
+def build_rotary_table(nc, pool):
+    partition = pool.tile([P, 1], I32)
+    nc.gpsimd.iota(partition[:], pattern=[[0, 1]], base=0, channel_multiplier=1)
+    position_int = pool.tile([P, 1], I32)
+    nc.vector.tensor_single_scalar(
+        out=position_int[:], in_=partition[:], scalar=1, op=ALU.arith_shift_right
+    )
+    position = pool.tile([P, 1], F32)
+    nc.vector.tensor_copy(out=position[:], in_=position_int[:])
+
+    ratio = ROPE_BASE ** (-1.0 / HALF)
+    frequency = pool.tile([P, HALF], F32)
+    nc.vector.memset(frequency[:, 0:1], 1.0)
+    filled = 1
+    while filled < HALF:
+        nc.vector.tensor_scalar_mul(
+            out=frequency[:, filled : 2 * filled],
+            in0=frequency[:, 0:filled],
+            scalar1=ratio**filled,
+        )
+        filled *= 2
+
+    angle = pool.tile([P, 3 * HALF], F32)
+    nc.vector.tensor_scalar(
+        out=angle[:, 0:HALF], in0=frequency[:], scalar1=position[:, 0:1],
+        scalar2=math.pi / 2.0, op0=ALU.mult, op1=ALU.add,
+    )
+    nc.vector.tensor_scalar(
+        out=angle[:, HALF : 2 * HALF], in0=frequency[:], scalar1=position[:, 0:1],
+        scalar2=-1.0, op0=ALU.mult, op1=ALU.mult,
+    )
+    nc.vector.tensor_scalar_mul(
+        out=angle[:, 2 * HALF : 3 * HALF], in0=frequency[:], scalar1=position[:, 0:1]
+    )
+
+    turns_int = pool.tile([P, 3 * HALF], I32)
+    nc.vector.tensor_scalar_mul(out=turns_int[:], in0=angle[:], scalar1=1.0 / (2.0 * math.pi))
+    turns = pool.tile([P, 3 * HALF], F32)
+    nc.vector.tensor_copy(out=turns[:], in_=turns_int[:])
+    for part_of_turn in (TURN_HI, TURN_LO):
+        nc.vector.scalar_tensor_tensor(
+            out=angle[:], in0=turns[:], scalar=-part_of_turn, in1=angle[:],
+            op0=ALU.mult, op1=ALU.add,
+        )
+    table = pool.tile([P, 3, HALF], F32)
+    nc.scalar.activation(
+        out=table[:].rearrange("r c d -> r (c d)"), in_=angle[:], func=ACT.Sin
+    )
+    return table
+
+
+def tile_attention_w_kernel(
+    tc, x, ln_gamma, ln_beta,
+    wq_words, wq_scales, wk_words, wk_scales, wv_words, wv_scales,
+    num_heads, out_0, out_1, out_2,
+):
+    nc = tc.nc
+    assert num_heads * HEAD == DM
+    all_words = (wq_words, wk_words, wv_words)
+    all_scales = (wq_scales, wk_scales, wv_scales)
+    outputs = (out_0, out_1, out_2)
+
+    with ExitStack() as stack:
+        keep = stack.enter_context(tc.tile_pool(name="keep", bufs=1))
+        work = stack.enter_context(tc.tile_pool(name="work", bufs=4))
+        psum = stack.enter_context(tc.psum_pool(name="psum", bufs=8))
+
+        x_sb = keep.tile([P, DM], BF16)
+        for b in range(B):
+            nc.sync.dma_start(out=x_sb[b:P:B, :], in_=x[b])
+        gamma_sb = keep.tile([P, G, PACK], BF16)
+        beta_sb = keep.tile([P, G, PACK], BF16)
+        nc.scalar.dma_start(out=gamma_sb[:], in_=ln_gamma.rearrange("(g q j) -> q g j", q=P, j=PACK))
+        nc.scalar.dma_start(out=beta_sb[:], in_=ln_beta.rearrange("(g q j) -> q g j", q=P, j=PACK))
+
+        planes = keep.tile([P, LAST_GROUP_SLOT + 1, DM], U8, align_bytes=64)
+        load_scale_planes(nc, planes, all_scales)
+
+        w_sb = []
+        for weight in range(3):
+            w_sb.append(keep.tile([P, G, DM], U32, name="w_sb%d" % weight, align_bytes=64))
+            for first, end in COLUMN_PARTS[weight]:
+                for g in range(G):
+                    nc.sync.dma_start(
+                        out=w_sb[weight][:, g, first:end].bitcast(I32),
+                        in_=all_words[weight][g, :, first:end, :]
+                        .rearrange("q n j -> q (n j)")
+                        .bitcast(I32),
+                    )
+
+        table = build_rotary_table(nc, keep)
+        cos = table[:, 0, :]
+        rotated_sin = table[:, 1:3, :]
+        identity = keep.tile([P, P], F32)
+        make_identity(nc, identity[:])
+
+        stats = keep.tile([P, G, 6], F32)
+        for g in range(G):
+            nc.vector.bn_stats(out=stats[:, g, :], in_=x_sb[:, K_PASS * g : K_PASS * (g + 1)])
+        mean_var = keep.tile([P, 2], F32)
+        nc.vector.bn_aggr(out=mean_var[:], in_=stats[:].rearrange("r g s -> r (g s)"))
+        spread = keep.tile([P, 1], F32)
+        nc.vector.tensor_scalar_add(out=spread[:], in0=mean_var[:, 1:2], scalar1=LN_EPS)
+        nc.scalar.sqrt(out=spread[:], in_=spread[:])
+        rstd = keep.tile([P, 1], F32)
+        nc.vector.reciprocal(out=rstd[:], in_=spread[:])
+        shift = keep.tile([P, 1], F32)
+        nc.vector.scalar_tensor_tensor(
+            out=shift[:], in0=mean_var[:, 0:1], scalar=-1.0, in1=rstd[:],
+            op0=ALU.mult, op1=ALU.mult,
+        )
+
+        x_words = keep.tile([P, G, P], U32, align_bytes=64)
+        x_scales = keep.tile([P, G, P], U8, align_bytes=64)
+        for g in range(G):
+            centred = work.tile([P, PACK, P], F32)
+            nc.scalar.activation(
+                out=centred[:],
+                in_=x_sb[:, K_PASS * g : K_PASS * (g + 1)].rearrange("r (q j) -> r j q", j=PACK),
+                func=ACT.Identity, scale=rstd[:, 0:1], bias=shift[:, 0:1],
+            )
+            transposed = psum.tile([P, PACK, P], F32, tag="bank")
+            for j in range(PACK):
+                nc.tensor.transpose(transposed[:, j, :], centred[:, j, :], identity[:])
+            scaled = work.tile([P, P, PACK], F32)
+            nc.vector.tensor_tensor(
+                out=scaled[:], in0=transposed[:].rearrange("q j r -> q r j"),
+                in1=gamma_sb[:, g, :].unsqueeze(1).to_broadcast([P, P, PACK]), op=ALU.mult,
+            )
+            xn = work.tile([P, P, PACK], BF16, align_bytes=64)
+            nc.vector.tensor_tensor(
+                out=xn[:], in0=scaled[:],
+                in1=beta_sb[:, g, :].unsqueeze(1).to_broadcast([P, P, PACK]), op=ALU.add,
+            )
+            nc.vector.quantize_mx(
+                out=x_words[:, g, :].bitcast(FP8X4), scales=x_scales[:, g, :],
+                in_=xn[:].rearrange("q r j -> q (r j)"),
+            )
+
+        for weight in range(3):
+            for first, end in COLUMN_PARTS[weight]:
+                banks = range(first, end, BANK)
+                acc = {n: psum.tile([P, BANK], F32, name="acc", tag="bank") for n in banks}
+                for g in range(G):
+                    for n in banks:
+                        nc.tensor.matmul_mx(
+                            out=acc[n][:],
+                            lhsT=x_words[:, g, :].bitcast(FP8X4),
+                            lhsT_scale=x_scales[:, g, :],
+                            rhs=w_sb[weight][:, g, n : n + BANK].bitcast(FP8X4),
+                            rhs_scale=scale_plane(planes, weight, g, slice(n, n + BANK)),
+                            start=(g == 0),
+                            stop=(g == G - 1),
+                        )
+                for n in banks:
+                    result = work.tile([P, HEADS_PER_BANK, 2, HALF], F32)
+                    if weight == 2:
+                        nc.scalar.copy(
+                            out=result[:].rearrange("r h s d -> r (h s d)"), in_=acc[n][:]
+                        )
+                    else:
+                        u = acc[n][:].rearrange("r (h s d) -> r h s d", s=2, d=HALF)
+                        nc.vector.tensor_tensor(
+                            out=result[:], in0=u,
+                            in1=cos.unsqueeze(1).unsqueeze(1).to_broadcast(
+                                [P, HEADS_PER_BANK, 2, HALF]
+                            ),
+                            op=ALU.mult,
+                        )
+                        crossed = work.tile([P, HEADS_PER_BANK, 2, HALF], F32)
+                        for s in range(2):
+                            nc.vector.tensor_tensor(
+                                out=crossed[:, :, s, :], in0=u[:, :, 1 - s, :],
+                                in1=rotated_sin[:, s, :].unsqueeze(1).to_broadcast(
+                                    [P, HEADS_PER_BANK, HALF]
+                                ),
+                                op=ALU.mult,
+                            )
+                        nc.vector.tensor_tensor(
+                            out=result[:], in0=result[:], in1=crossed[:], op=ALU.add
+                        )
+                    head = n // HEAD
+                    for b in range(B):
+                        nc.scalar.dma_start(
+                            out=outputs[weight][b, head : head + HEADS_PER_BANK].rearrange(
+                                "h t d -> t h d"
+                            ),
+                            in_=result[b:P:B].rearrange("r h s d -> r h (s d)"),
+                        )

@@ -48,18 +48,18 @@ def scale_plane(planes, weight, g, columns):
 
 def load_scale_planes(nc, planes, all_scales):
     nc.vector.memset(planes[:].bitcast(I32), 0)
-    for quadrant in range(QUADRANTS):
-        rows = slice(PLANE_ROWS * quadrant, PLANE_ROWS * (quadrant + 1))
-        first = 32 * quadrant
-        for weight, scales in enumerate(all_scales):
-            nc.sync.dma_start(
-                out=planes[first : first + PLANES_PER_SLOT * PLANE_ROWS, weight, :].bitcast(I32),
-                in_=scales[0:PLANES_PER_SLOT, rows, :].bitcast(I32),
+    for weight, scales in enumerate(all_scales):
+        for quadrant in range(QUADRANTS):
+            rows = slice(PLANE_ROWS * quadrant, PLANE_ROWS * (quadrant + 1))
+            first = 32 * quadrant
+            nc.gpsimd.dma_start(
+                out=planes[first : first + PLANES_PER_SLOT * PLANE_ROWS, weight, :].bitcast(F32),
+                in_=scales[0:PLANES_PER_SLOT, rows, :].bitcast(F32),
             )
             mine = first + PLANE_ROWS * weight
-            nc.sync.dma_start(
-                out=planes[mine : mine + PLANE_ROWS, LAST_GROUP_SLOT, :].bitcast(I32),
-                in_=scales[PLANES_PER_SLOT, rows, :].bitcast(I32),
+            nc.gpsimd.dma_start(
+                out=planes[mine : mine + PLANE_ROWS, LAST_GROUP_SLOT, :].bitcast(F32),
+                in_=scales[PLANES_PER_SLOT, rows, :].bitcast(F32),
             )
 
 

@@ -130,6 +130,12 @@ def tile_attention_w_kernel(
         work = stack.enter_context(tc.tile_pool(name="work", bufs=4))
         psum = stack.enter_context(tc.psum_pool(name="psum", bufs=8))
 
+        table = build_rotary_table(nc, keep)
+        cos = table[:, 0, :]
+        rotated_sin = table[:, 1:3, :]
+        identity = keep.tile([P, P], F32)
+        make_identity(nc, identity[:])
+
         x_sb = keep.tile([P, DM], BF16)
         for b in range(B):
             nc.sync.dma_start(out=x_sb[b:P:B, :], in_=x[b])
@@ -152,12 +158,6 @@ def tile_attention_w_kernel(
                         .rearrange("q n j -> q (n j)")
                         .bitcast(I32),
                     )
-
-        table = build_rotary_table(nc, keep)
-        cos = table[:, 0, :]
-        rotated_sin = table[:, 1:3, :]
-        identity = keep.tile([P, P], F32)
-        make_identity(nc, identity[:])
 
         stats = keep.tile([P, G, 6], F32)
         for g in range(G):

@@ -33,7 +33,6 @@ LAST_GROUP_SLOT = 3
 TURN_HI = 6.28125
 TURN_LO = 2.0 * math.pi - TURN_HI
 
-COLUMN_PARTS = (((0, DM),), ((0, DM),), ((0, DM - BANK), (DM - BANK, DM)))
 
 FLOPS = 2 * P * DM * 3 * DM
 
@@ -127,7 +126,8 @@ def tile_attention_w_kernel(
 
     with ExitStack() as stack:
         keep = stack.enter_context(tc.tile_pool(name="keep", bufs=1))
-        work = stack.enter_context(tc.tile_pool(name="work", bufs=4))
+        work = stack.enter_context(tc.tile_pool(name="work", bufs=3))
+        stack.enter_context(tc.manual_schedule(engines={mybir.EngineType.SP}))
         psum = stack.enter_context(tc.psum_pool(name="psum", bufs=8))
 
         table = build_rotary_table(nc, keep)
@@ -150,14 +150,11 @@ def tile_attention_w_kernel(
         w_sb = []
         for weight in range(3):
             w_sb.append(keep.tile([P, G, DM], U32, name="w_sb%d" % weight, align_bytes=64))
-            for first, end in COLUMN_PARTS[weight]:
-                for g in range(G):
-                    nc.sync.dma_start(
-                        out=w_sb[weight][:, g, first:end].bitcast(I32),
-                        in_=all_words[weight][g, :, first:end, :]
-                        .rearrange("q n j -> q (n j)")
-                        .bitcast(I32),
-                    )
+            for g in range(G):
+                nc.sync.dma_start(
+                    out=w_sb[weight][:, g, :].bitcast(I32),
+                    in_=all_words[weight][g].rearrange("q n j -> q (n j)").bitcast(I32),
+                )
 
         stats = keep.tile([P, G, 6], F32)
         for g in range(G):
@@ -202,53 +199,48 @@ def tile_attention_w_kernel(
                 in_=xn[:].rearrange("q r j -> q (r j)"),
             )
 
+        banks = range(0, DM, BANK)
         for weight in range(3):
-            for first, end in COLUMN_PARTS[weight]:
-                banks = range(first, end, BANK)
-                acc = {n: psum.tile([P, BANK], F32, name="acc", tag="bank") for n in banks}
-                for g in range(G):
-                    for n in banks:
-                        nc.tensor.matmul_mx(
-                            out=acc[n][:],
-                            lhsT=x_words[:, g, :].bitcast(FP8X4),
-                            lhsT_scale=x_scales[:, g, :],
-                            rhs=w_sb[weight][:, g, n : n + BANK].bitcast(FP8X4),
-                            rhs_scale=scale_plane(planes, weight, g, slice(n, n + BANK)),
-                            start=(g == 0),
-                            stop=(g == G - 1),
-                        )
+            acc = {n: psum.tile([P, BANK], F32, name="acc", tag="bank") for n in banks}
+            for g in range(G):
                 for n in banks:
-                    result = work.tile([P, HEADS_PER_BANK, 2, HALF], F32)
-                    if weight == 2:
-                        nc.scalar.copy(
-                            out=result[:].rearrange("r h s d -> r (h s d)"), in_=acc[n][:]
-                        )
+                    nc.tensor.matmul_mx(
+                        out=acc[n][:],
+                        lhsT=x_words[:, g, :].bitcast(FP8X4),
+                        lhsT_scale=x_scales[:, g, :],
+                        rhs=w_sb[weight][:, g, n : n + BANK].bitcast(FP8X4),
+                        rhs_scale=scale_plane(planes, weight, g, slice(n, n + BANK)),
+                        start=(g == 0),
+                        stop=(g == G - 1),
+                    )
+            whole = keep.tile([P, DM], F32, name="whole%d" % weight)
+            for turn, n in enumerate(banks):
+                flat = whole[:, n : n + BANK]
+                if weight == 2:
+                    if turn % 2 == 0:
+                        nc.scalar.copy(out=flat, in_=acc[n][:])
                     else:
-                        u = acc[n][:].rearrange("r (h s d) -> r h s d", s=2, d=HALF)
-                        nc.vector.tensor_tensor(
-                            out=result[:], in0=u,
-                            in1=cos.unsqueeze(1).unsqueeze(1).to_broadcast(
-                                [P, HEADS_PER_BANK, 2, HALF]
-                            ),
-                            op=ALU.mult,
-                        )
-                        crossed = work.tile([P, HEADS_PER_BANK, 2, HALF], F32)
-                        for s in range(2):
-                            nc.vector.tensor_tensor(
-                                out=crossed[:, :, s, :], in0=u[:, :, 1 - s, :],
-                                in1=rotated_sin[:, s, :].unsqueeze(1).to_broadcast(
-                                    [P, HEADS_PER_BANK, HALF]
-                                ),
-                                op=ALU.mult,
-                            )
-                        nc.vector.tensor_tensor(
-                            out=result[:], in0=result[:], in1=crossed[:], op=ALU.add
-                        )
-                    head = n // HEAD
-                    for b in range(B):
-                        nc.scalar.dma_start(
-                            out=outputs[weight][b, head : head + HEADS_PER_BANK].rearrange(
-                                "h t d -> t h d"
-                            ),
-                            in_=result[b:P:B].rearrange("r h s d -> r h (s d)"),
-                        )
+                        nc.vector.tensor_copy(out=flat, in_=acc[n][:])
+                    continue
+                result = flat.rearrange("r (h s d) -> r h s d", s=2, d=HALF)
+                u = acc[n][:].rearrange("r (h s d) -> r h s d", s=2, d=HALF)
+                nc.vector.tensor_tensor(
+                    out=result, in0=u,
+                    in1=cos.unsqueeze(1).unsqueeze(1).to_broadcast([P, HEADS_PER_BANK, 2, HALF]),
+                    op=ALU.mult,
+                )
+                crossed = work.tile([P, HEADS_PER_BANK, 2, HALF], F32)
+                for s in range(2):
+                    nc.vector.tensor_tensor(
+                        out=crossed[:, :, s, :], in0=u[:, :, 1 - s, :],
+                        in1=rotated_sin[:, s, :].unsqueeze(1).to_broadcast(
+                            [P, HEADS_PER_BANK, HALF]
+                        ),
+                        op=ALU.mult,
+                    )
+                nc.vector.tensor_tensor(out=result, in0=result, in1=crossed[:], op=ALU.add)
+            for b in range(B):
+                nc.sync.dma_start(
+                    out=outputs[weight][b].rearrange("h t d -> t h d"),
+                    in_=whole[b:P:B, :].rearrange("r (h d) -> r h d", d=HEAD),
+                )

@@ -139,10 +139,10 @@ def tile_attention_w_kernel(
         x_sb = keep.tile([P, DM], BF16)
         for b in range(B):
             nc.sync.dma_start(out=x_sb[b:P:B, :], in_=x[b])
-        gamma_sb = keep.tile([P, G, PACK], BF16)
-        beta_sb = keep.tile([P, G, PACK], BF16)
-        nc.scalar.dma_start(out=gamma_sb[:], in_=ln_gamma.rearrange("(g q j) -> q g j", q=P, j=PACK))
-        nc.scalar.dma_start(out=beta_sb[:], in_=ln_beta.rearrange("(g q j) -> q g j", q=P, j=PACK))
+        rows = keep.tile([P, K_PASS], BF16)
+        nc.vector.memset(rows[:], 0.0)
+        nc.scalar.dma_start(out=rows[0:G, :], in_=ln_gamma.rearrange("(g c) -> g c", g=G))
+        nc.scalar.dma_start(out=rows[G : 2 * G, :], in_=ln_beta.rearrange("(g c) -> g c", g=G))
 
         planes = keep.tile([P, LAST_GROUP_SLOT + 1, DM], U8, align_bytes=64)
         load_scale_planes(nc, planes, all_scales)
@@ -155,6 +155,16 @@ def tile_attention_w_kernel(
                     out=w_sb[weight][:, g, :].bitcast(I32),
                     in_=all_words[weight][g].rearrange("q n j -> q (n j)").bitcast(I32),
                 )
+
+        sorted_rows = keep.tile([P, PACK, P], F32)
+        nc.vector.tensor_copy(out=sorted_rows[:], in_=rows[:].rearrange("r (q j) -> r j q", j=PACK))
+        turned = psum.tile([P, PACK, P], F32, tag="bank")
+        for j in range(PACK):
+            nc.tensor.transpose(turned[:, j, :], sorted_rows[:, j, :], identity[:])
+        gamma_beta = keep.tile([P, 2 * G, PACK], F32)
+        nc.vector.tensor_copy(
+            out=gamma_beta[:], in_=turned[:, :, 0 : 2 * G].rearrange("q j r -> q r j")
+        )
 
         stats = keep.tile([P, G, 6], F32)
         for g in range(G):
@@ -187,12 +197,12 @@ def tile_attention_w_kernel(
             scaled = work.tile([P, P, PACK], F32)
             nc.vector.tensor_tensor(
                 out=scaled[:], in0=transposed[:].rearrange("q j r -> q r j"),
-                in1=gamma_sb[:, g, :].unsqueeze(1).to_broadcast([P, P, PACK]), op=ALU.mult,
+                in1=gamma_beta[:, g, :].unsqueeze(1).to_broadcast([P, P, PACK]), op=ALU.mult,
             )
             xn = work.tile([P, P, PACK], BF16, align_bytes=64)
             nc.vector.tensor_tensor(
                 out=xn[:], in0=scaled[:],
-                in1=beta_sb[:, g, :].unsqueeze(1).to_broadcast([P, P, PACK]), op=ALU.add,
+                in1=gamma_beta[:, G + g, :].unsqueeze(1).to_broadcast([P, P, PACK]), op=ALU.add,
             )
             nc.vector.quantize_mx(
                 out=x_words[:, g, :].bitcast(FP8X4), scales=x_scales[:, g, :],

@@ -249,8 +249,4 @@ def tile_attention_w_kernel(
                         op=ALU.mult,
                     )
                 nc.vector.tensor_tensor(out=result, in0=result, in1=crossed[:], op=ALU.add)
-            for b in range(B):
-                nc.sync.dma_start(
-                    out=outputs[weight][b].rearrange("h t d -> t h d"),
-                    in_=whole[b:P:B, :].rearrange("r (h d) -> r h d", d=HEAD),
-                )
+            nc.sync.dma_start(out=outputs[weight].rearrange("b h t d -> t (b h) d"), in_=whole[:])

@@ -25,10 +25,10 @@ HEADS_PER_BANK = BANK // HEAD
 LN_EPS = 1e-5
 ROPE_BASE = 10000.0
 
-QUADRANTS = 4
 PLANE_ROWS = 4
 PLANES_PER_SLOT = 4
-LAST_GROUP_SLOT = 3
+LAST_STEP = BANK + 64
+QUADRANT_ORDER = (0, 2, 1, 3)
 
 TURN_HI = 6.28125
 TURN_LO = 2.0 * math.pi - TURN_HI
@@ -37,18 +37,17 @@ TURN_LO = 2.0 * math.pi - TURN_HI
 FLOPS = 2 * P * DM * 3 * DM
 
 
-def scale_plane(planes, weight, g, columns):
+def scale_plane(planes, last_planes, weight, g, n):
     if g < PLANES_PER_SLOT:
-        first_row, slot = PLANE_ROWS * g, weight
-    else:
-        first_row, slot = PLANE_ROWS * weight, LAST_GROUP_SLOT
-    return planes[first_row:P, slot, columns]
+        return planes[PLANE_ROWS * g : P, weight, n : n + BANK]
+    return last_planes[PLANE_ROWS * weight : P, n // BANK, 0:BANK]
 
 
-def load_scale_planes(nc, planes, all_scales):
+def load_scale_planes(nc, planes, last_planes, all_scales):
     nc.vector.memset(planes[:].bitcast(I32), 0)
+    nc.vector.memset(last_planes[:].bitcast(I32), 0)
     for weight, scales in enumerate(all_scales):
-        for quadrant in range(QUADRANTS):
+        for quadrant in QUADRANT_ORDER:
             rows = slice(PLANE_ROWS * quadrant, PLANE_ROWS * (quadrant + 1))
             first = 32 * quadrant
             nc.gpsimd.dma_start(
@@ -57,8 +56,10 @@ def load_scale_planes(nc, planes, all_scales):
             )
             mine = first + PLANE_ROWS * weight
             nc.gpsimd.dma_start(
-                out=planes[mine : mine + PLANE_ROWS, LAST_GROUP_SLOT, :].bitcast(F32),
-                in_=scales[PLANES_PER_SLOT, rows, :].bitcast(F32),
+                out=last_planes[mine : mine + PLANE_ROWS, :, 0:BANK].bitcast(F32),
+                in_=scales[PLANES_PER_SLOT, rows, :]
+                .rearrange("r (c n) -> r c n", n=BANK)
+                .bitcast(F32),
             )
 
 
@@ -144,8 +145,9 @@ def tile_attention_w_kernel(
         nc.scalar.dma_start(out=rows[0:G, :], in_=ln_gamma.rearrange("(g c) -> g c", g=G))
         nc.scalar.dma_start(out=rows[G : 2 * G, :], in_=ln_beta.rearrange("(g c) -> g c", g=G))
 
-        planes = keep.tile([P, LAST_GROUP_SLOT + 1, DM], U8, align_bytes=64)
-        load_scale_planes(nc, planes, all_scales)
+        planes = keep.tile([P, 3, DM], U8, align_bytes=64)
+        last_planes = keep.tile([P, DM // BANK, LAST_STEP], U8, align_bytes=64)
+        load_scale_planes(nc, planes, last_planes, all_scales)
 
         w_sb = []
         for weight in range(3):
@@ -219,7 +221,7 @@ def tile_attention_w_kernel(
                         lhsT=x_words[:, g, :].bitcast(FP8X4),
                         lhsT_scale=x_scales[:, g, :],
                         rhs=w_sb[weight][:, g, n : n + BANK].bitcast(FP8X4),
-                        rhs_scale=scale_plane(planes, weight, g, slice(n, n + BANK)),
+                        rhs_scale=scale_plane(planes, last_planes, weight, g, n),
                         start=(g == 0),
                         stop=(g == G - 1),
                     )

@@ -138,8 +138,7 @@ def tile_attention_w_kernel(
         make_identity(nc, identity[:])
 
         x_sb = keep.tile([P, DM], BF16)
-        for b in range(B):
-            nc.sync.dma_start(out=x_sb[b:P:B, :], in_=x[b])
+        nc.sync.dma_start(out=x_sb[:], in_=x.rearrange("b t k -> (b t) k"))
         rows = keep.tile([P, K_PASS], BF16)
         nc.vector.memset(rows[:], 0.0)
         nc.scalar.dma_start(out=rows[0:G, :], in_=ln_gamma.rearrange("(g c) -> g c", g=G))
@@ -198,8 +197,10 @@ def tile_attention_w_kernel(
                 nc.tensor.transpose(transposed[:, j, :], centred[:, j, :], identity[:])
             scaled = work.tile([P, P, PACK], F32)
             nc.vector.tensor_tensor(
-                out=scaled[:], in0=transposed[:].rearrange("q j r -> q r j"),
-                in1=gamma_beta[:, g, :].unsqueeze(1).to_broadcast([P, P, PACK]), op=ALU.mult,
+                out=scaled[:].rearrange("q (t b) j -> q b t j", b=B),
+                in0=transposed[:].rearrange("q j (b t) -> q b t j", b=B),
+                in1=gamma_beta[:, g, :].unsqueeze(1).unsqueeze(1).to_broadcast([P, B, T, PACK]),
+                op=ALU.mult,
             )
             xn = work.tile([P, P, PACK], BF16, align_bytes=64)
             nc.vector.tensor_tensor(

@@ -150,7 +150,7 @@ def tile_attention_w_kernel(
 
         w_sb = []
         for weight in range(3):
-            w_sb.append(keep.tile([P, G, DM], U32, name="w_sb%d" % weight, align_bytes=64))
+            w_sb.append(keep.tile([P, G, DM], U32, name="w_sb%d" % weight, align_bytes=256))
             for g in range(G):
                 nc.sync.dma_start(
                     out=w_sb[weight][:, g, :].bitcast(I32),
@@ -226,7 +226,7 @@ def tile_attention_w_kernel(
                         start=(g == 0),
                         stop=(g == G - 1),
                     )
-            whole = keep.tile([P, DM], F32, name="whole%d" % weight)
+            whole = keep.tile([P, DM], F32, name="whole%d" % weight, align_bytes=256)
             for turn, n in enumerate(banks):
                 flat = whole[:, n : n + BANK]
                 if weight == 2:

@@ -27,7 +27,7 @@ ROPE_BASE = 10000.0
 
 PLANE_ROWS = 4
 PLANES_PER_SLOT = 4
-LAST_STEP = BANK + 64
+LAST_STEP = BANK + 256
 QUADRANT_ORDER = (0, 2, 1, 3)
 
 TURN_HI = 6.28125
@@ -137,15 +137,15 @@ def tile_attention_w_kernel(
         identity = keep.tile([P, P], F32)
         make_identity(nc, identity[:])
 
-        x_sb = keep.tile([P, DM], BF16)
+        x_sb = keep.tile([P, DM], BF16, align_bytes=256)
         nc.sync.dma_start(out=x_sb[:], in_=x.rearrange("b t k -> (b t) k"))
         rows = keep.tile([P, K_PASS], BF16)
         nc.vector.memset(rows[:], 0.0)
         nc.scalar.dma_start(out=rows[0:G, :], in_=ln_gamma.rearrange("(g c) -> g c", g=G))
         nc.scalar.dma_start(out=rows[G : 2 * G, :], in_=ln_beta.rearrange("(g c) -> g c", g=G))
 
-        planes = keep.tile([P, 3, DM], U8, align_bytes=64)
-        last_planes = keep.tile([P, DM // BANK, LAST_STEP], U8, align_bytes=64)
+        planes = keep.tile([P, 3, DM], U8, align_bytes=256)
+        last_planes = keep.tile([P, DM // BANK, LAST_STEP], U8, align_bytes=256)
         load_scale_planes(nc, planes, last_planes, all_scales)
 
         w_sb = []

@@ -27,8 +27,11 @@ ROPE_BASE = 10000.0
 
 PLANE_ROWS = 4
 PLANES_PER_SLOT = 4
-LAST_STEP = BANK + 256
-QUADRANT_ORDER = (0, 2, 1, 3)
+SLOT_ROWS = PLANES_PER_SLOT * PLANE_ROWS
+SHARED = PLANES_PER_SLOT * BANK
+SYNC_QUADRANTS = (0, 1)
+GPSIMD_QUADRANTS = (2, 3)
+FILLER = 64
 
 TURN_HI = 6.28125
 TURN_LO = 2.0 * math.pi - TURN_HI
@@ -37,30 +40,48 @@ TURN_LO = 2.0 * math.pi - TURN_HI
 FLOPS = 2 * P * DM * 3 * DM
 
 
-def scale_plane(planes, last_planes, weight, g, n):
-    if g < PLANES_PER_SLOT:
-        return planes[PLANE_ROWS * g : P, weight, n : n + BANK]
-    return last_planes[PLANE_ROWS * weight : P, n // BANK, 0:BANK]
+def scale_dmas(planes, last_planes, scales, weight, quadrant, dtype):
+    rows = slice(PLANE_ROWS * quadrant, PLANE_ROWS * (quadrant + 1))
+    mine = slice(32 * quadrant, 32 * quadrant + SLOT_ROWS)
+    return [
+        (
+            planes[mine, weight, :].bitcast(dtype),
+            scales[0:PLANES_PER_SLOT, rows, :].bitcast(dtype),
+        ),
+        (
+            last_planes[mine, weight, 0:BANK].bitcast(dtype),
+            scales[PLANES_PER_SLOT, rows, 0:SHARED]
+            .rearrange("r (c n) -> c r n", n=BANK)
+            .bitcast(dtype),
+        ),
+        (
+            last_planes[mine.start : mine.start + PLANE_ROWS, weight, BANK : 2 * BANK].bitcast(dtype),
+            scales[PLANES_PER_SLOT, rows, SHARED:DM].bitcast(dtype),
+        ),
+    ]
 
 
-def load_scale_planes(nc, planes, last_planes, all_scales):
-    nc.vector.memset(planes[:].bitcast(I32), 0)
-    nc.vector.memset(last_planes[:].bitcast(I32), 0)
-    for weight, scales in enumerate(all_scales):
-        for quadrant in QUADRANT_ORDER:
-            rows = slice(PLANE_ROWS * quadrant, PLANE_ROWS * (quadrant + 1))
-            first = 32 * quadrant
-            nc.gpsimd.dma_start(
-                out=planes[first : first + PLANES_PER_SLOT * PLANE_ROWS, weight, :].bitcast(F32),
-                in_=scales[0:PLANES_PER_SLOT, rows, :].bitcast(F32),
-            )
-            mine = first + PLANE_ROWS * weight
-            nc.gpsimd.dma_start(
-                out=last_planes[mine : mine + PLANE_ROWS, :, 0:BANK].bitcast(F32),
-                in_=scales[PLANES_PER_SLOT, rows, :]
-                .rearrange("r (c n) -> r c n", n=BANK)
-                .bitcast(F32),
-            )
+def load_scales_on_gpsimd(nc, planes, last_planes, spare, all_scales):
+    def turn(count, place):
+        half = FILLER // 2
+        nc.gpsimd.dma_start(
+            out=spare[0:count, place, :, 0:half].bitcast(F32),
+            in_=all_scales[0][0, 0:count, 0:FILLER]
+            .rearrange("r (c n) -> r c n", n=half)
+            .bitcast(F32),
+        )
+
+    dmas = [
+        dma
+        for weight, scales in enumerate(all_scales)
+        for part in range(2)
+        for quadrant in GPSIMD_QUADRANTS
+        for dma in [scale_dmas(planes, last_planes, scales, weight, quadrant, F32)[part]]
+    ]
+    turn(8, 0)
+    for i, (out, in_) in enumerate(dmas):
+        nc.gpsimd.dma_start(out=out, in_=in_)
+        turn(12 if i + 1 < len(dmas) else 4, i + 1)
 
 
 def build_rotary_table(nc, pool):
@@ -128,7 +149,9 @@ def tile_attention_w_kernel(
     with ExitStack() as stack:
         keep = stack.enter_context(tc.tile_pool(name="keep", bufs=1))
         work = stack.enter_context(tc.tile_pool(name="work", bufs=3))
-        stack.enter_context(tc.manual_schedule(engines={mybir.EngineType.SP}))
+        stack.enter_context(
+            tc.manual_schedule(engines={mybir.EngineType.SP, mybir.EngineType.Pool})
+        )
         psum = stack.enter_context(tc.psum_pool(name="psum", bufs=8))
 
         table = build_rotary_table(nc, keep)
@@ -145,17 +168,29 @@ def tile_attention_w_kernel(
         nc.scalar.dma_start(out=rows[G : 2 * G, :], in_=ln_beta.rearrange("(g c) -> g c", g=G))
 
         planes = keep.tile([P, 3, DM], U8, align_bytes=256)
-        last_planes = keep.tile([P, DM // BANK, LAST_STEP], U8, align_bytes=256)
-        load_scale_planes(nc, planes, last_planes, all_scales)
+        last_planes = keep.tile([P, 3, 2 * BANK], U8, align_bytes=256)
+        nc.vector.memset(planes[:].bitcast(I32), 0)
+        nc.vector.memset(last_planes[:].bitcast(I32), 0)
+        spare = keep.tile([P, 13, 2, FILLER], U8)
+        load_scales_on_gpsimd(nc, planes, last_planes, spare, all_scales)
 
         w_sb = []
         for weight in range(3):
             w_sb.append(keep.tile([P, G, DM], U32, name="w_sb%d" % weight, align_bytes=256))
+            by_quadrant = [
+                scale_dmas(planes, last_planes, all_scales[weight], weight, quadrant, I32)
+                for quadrant in range(4)
+            ]
+            small = [by_quadrant[quadrant][part] for part in range(2) for quadrant in SYNC_QUADRANTS]
+            small += [dmas[2] for dmas in by_quadrant]
             for g in range(G):
                 nc.sync.dma_start(
                     out=w_sb[weight][:, g, :].bitcast(I32),
                     in_=all_words[weight][g].rearrange("q n j -> q (n j)").bitcast(I32),
                 )
+                if g > 0:
+                    for out, in_ in small[2 * g - 2 : 2 * g]:
+                        nc.sync.dma_start(out=out, in_=in_)
 
         sorted_rows = keep.tile([P, PACK, P], F32)
         nc.vector.tensor_copy(out=sorted_rows[:], in_=rows[:].rearrange("r (q j) -> r j q", j=PACK))
@@ -217,12 +252,18 @@ def tile_attention_w_kernel(
             acc = {n: psum.tile([P, BANK], F32, name="acc", tag="bank") for n in banks}
             for g in range(G):
                 for n in banks:
+                    if g < PLANES_PER_SLOT:
+                        scale = planes[PLANE_ROWS * g : P, weight, n : n + BANK]
+                    elif n < SHARED:
+                        scale = last_planes[PLANE_ROWS * (n // BANK) : P, weight, 0:BANK]
+                    else:
+                        scale = last_planes[0:P, weight, BANK : 2 * BANK]
                     nc.tensor.matmul_mx(
                         out=acc[n][:],
                         lhsT=x_words[:, g, :].bitcast(FP8X4),
                         lhsT_scale=x_scales[:, g, :],
                         rhs=w_sb[weight][:, g, n : n + BANK].bitcast(FP8X4),
-                        rhs_scale=scale_plane(planes, last_planes, weight, g, n),
+                        rhs_scale=scale,
                         start=(g == 0),
                         stop=(g == G - 1),
                     )

@@ -22,6 +22,7 @@ HEAD = 128
 HALF = HEAD // 2
 BANK = 512
 HEADS_PER_BANK = BANK // HEAD
+LAST_PART = 3 * BANK
 LN_EPS = 1e-5
 ROPE_BASE = 10000.0
 
@@ -184,10 +185,14 @@ def tile_attention_w_kernel(
             small = [by_quadrant[quadrant][part] for part in range(2) for quadrant in SYNC_QUADRANTS]
             small += [dmas[2] for dmas in by_quadrant]
             for g in range(G):
-                nc.sync.dma_start(
-                    out=w_sb[weight][:, g, :].bitcast(I32),
-                    in_=all_words[weight][g].rearrange("q n j -> q (n j)").bitcast(I32),
-                )
+                last = weight == 2 and g == G - 1
+                for first, end in ((0, LAST_PART), (LAST_PART, DM)) if last else ((0, DM),):
+                    nc.sync.dma_start(
+                        out=w_sb[weight][:, g, first:end].bitcast(I32),
+                        in_=all_words[weight][g, :, first:end, :]
+                        .rearrange("q n j -> q (n j)")
+                        .bitcast(I32),
+                    )
                 if g > 0:
                     for out, in_ in small[2 * g - 2 : 2 * g]:
                         nc.sync.dma_start(out=out, in_=in_)

@@ -161,7 +161,7 @@ def tile_attention_w_kernel(
         identity = keep.tile([P, P], F32)
         make_identity(nc, identity[:])
 
-        x_sb = keep.tile([P, DM], BF16, align_bytes=256)
+        x_sb = keep.tile([P, DM], BF16, align_bytes=1024)
         nc.sync.dma_start(out=x_sb[:], in_=x.rearrange("b t k -> (b t) k"))
         rows = keep.tile([P, K_PASS], BF16)
         nc.vector.memset(rows[:], 0.0)
@@ -177,7 +177,7 @@ def tile_attention_w_kernel(
 
         w_sb = []
         for weight in range(3):
-            w_sb.append(keep.tile([P, G, DM], U32, name="w_sb%d" % weight, align_bytes=256))
+            w_sb.append(keep.tile([P, G, DM], U32, name="w_sb%d" % weight, align_bytes=1024))
             by_quadrant = [
                 scale_dmas(planes, last_planes, all_scales[weight], weight, quadrant, I32)
                 for quadrant in range(4)
@@ -272,7 +272,7 @@ def tile_attention_w_kernel(
                         start=(g == 0),
                         stop=(g == G - 1),
                     )
-            whole = keep.tile([P, DM], F32, name="whole%d" % weight, align_bytes=256)
+            whole = keep.tile([P, DM], F32, name="whole%d" % weight, align_bytes=1024)
             for turn, n in enumerate(banks):
                 flat = whole[:, n : n + BANK]
                 if weight == 2:

import math
from contextlib import ExitStack

import concourse.mybir as mybir
from concourse.masks import make_identity

F32 = mybir.dt.float32
BF16 = mybir.dt.bfloat16
I32 = mybir.dt.int32
U32 = mybir.dt.uint32
U8 = mybir.dt.uint8
FP8X4 = mybir.dt.float8_e4m3fn_x4
ALU = mybir.AluOpType
ACT = mybir.ActivationFunctionType

P = 128
B, T, DM = 2, 64, 2560
PACK = 4
K_PASS = P * PACK
G = DM // K_PASS
HEAD = 128
HALF = HEAD // 2
BANK = 512
HEADS_PER_BANK = BANK // HEAD
LAST_PART = 3 * BANK
LN_EPS = 1e-5
ROPE_BASE = 10000.0

PLANE_ROWS = 4
PLANES_PER_SLOT = 4
SLOT_ROWS = PLANES_PER_SLOT * PLANE_ROWS
SHARED = PLANES_PER_SLOT * BANK
SYNC_QUADRANTS = (0, 1)
GPSIMD_QUADRANTS = (2, 3)
FILLER = 64

TURN_HI = 6.28125
TURN_LO = 2.0 * math.pi - TURN_HI


FLOPS = 2 * P * DM * 3 * DM


def scale_dmas(planes, last_planes, scales, weight, quadrant, dtype):
    rows = slice(PLANE_ROWS * quadrant, PLANE_ROWS * (quadrant + 1))
    mine = slice(32 * quadrant, 32 * quadrant + SLOT_ROWS)
    return [
        (
            planes[mine, weight, :].bitcast(dtype),
            scales[0:PLANES_PER_SLOT, rows, :].bitcast(dtype),
        ),
        (
            last_planes[mine, weight, 0:BANK].bitcast(dtype),
            scales[PLANES_PER_SLOT, rows, 0:SHARED]
            .rearrange("r (c n) -> c r n", n=BANK)
            .bitcast(dtype),
        ),
        (
            last_planes[mine.start : mine.start + PLANE_ROWS, weight, BANK : 2 * BANK].bitcast(dtype),
            scales[PLANES_PER_SLOT, rows, SHARED:DM].bitcast(dtype),
        ),
    ]


def load_scales_on_gpsimd(nc, planes, last_planes, spare, all_scales):
    def turn(count, place):
        half = FILLER // 2
        nc.gpsimd.dma_start(
            out=spare[0:count, place, :, 0:half].bitcast(F32),
            in_=all_scales[0][0, 0:count, 0:FILLER]
            .rearrange("r (c n) -> r c n", n=half)
            .bitcast(F32),
        )

    dmas = [
        dma
        for weight, scales in enumerate(all_scales)
        for part in range(2)
        for quadrant in GPSIMD_QUADRANTS
        for dma in [scale_dmas(planes, last_planes, scales, weight, quadrant, F32)[part]]
    ]
    turn(8, 0)
    for i, (out, in_) in enumerate(dmas):
        nc.gpsimd.dma_start(out=out, in_=in_)
        turn(12 if i + 1 < len(dmas) else 4, i + 1)


def build_rotary_table(nc, pool):
    partition = pool.tile([P, 1], I32)
    nc.gpsimd.iota(partition[:], pattern=[[0, 1]], base=0, channel_multiplier=1)
    position_int = pool.tile([P, 1], I32)
    nc.vector.tensor_single_scalar(
        out=position_int[:], in_=partition[:], scalar=1, op=ALU.arith_shift_right
    )
    position = pool.tile([P, 1], F32)
    nc.vector.tensor_copy(out=position[:], in_=position_int[:])

    ratio = ROPE_BASE ** (-1.0 / HALF)
    frequency = pool.tile([P, HALF], F32)
    nc.vector.memset(frequency[:, 0:1], 1.0)
    filled = 1
    while filled < HALF:
        nc.vector.tensor_scalar_mul(
            out=frequency[:, filled : 2 * filled],
            in0=frequency[:, 0:filled],
            scalar1=ratio**filled,
        )
        filled *= 2

    angle = pool.tile([P, 3 * HALF], F32)
    nc.vector.tensor_scalar(
        out=angle[:, 0:HALF], in0=frequency[:], scalar1=position[:, 0:1],
        scalar2=math.pi / 2.0, op0=ALU.mult, op1=ALU.add,
    )
    nc.vector.tensor_scalar(
        out=angle[:, HALF : 2 * HALF], in0=frequency[:], scalar1=position[:, 0:1],
        scalar2=-1.0, op0=ALU.mult, op1=ALU.mult,
    )
    nc.vector.tensor_scalar_mul(
        out=angle[:, 2 * HALF : 3 * HALF], in0=frequency[:], scalar1=position[:, 0:1]
    )

    turns_int = pool.tile([P, 3 * HALF], I32)
    nc.vector.tensor_scalar_mul(out=turns_int[:], in0=angle[:], scalar1=1.0 / (2.0 * math.pi))
    turns = pool.tile([P, 3 * HALF], F32)
    nc.vector.tensor_copy(out=turns[:], in_=turns_int[:])
    for part_of_turn in (TURN_HI, TURN_LO):
        nc.vector.scalar_tensor_tensor(
            out=angle[:], in0=turns[:], scalar=-part_of_turn, in1=angle[:],
            op0=ALU.mult, op1=ALU.add,
        )
    table = pool.tile([P, 3, HALF], F32)
    nc.scalar.activation(
        out=table[:].rearrange("r c d -> r (c d)"), in_=angle[:], func=ACT.Sin
    )
    return table


def tile_attention_w_kernel(
    tc, x, ln_gamma, ln_beta,
    wq_words, wq_scales, wk_words, wk_scales, wv_words, wv_scales,
    num_heads, out_0, out_1, out_2,
):
    nc = tc.nc
    assert num_heads * HEAD == DM
    all_words = (wq_words, wk_words, wv_words)
    all_scales = (wq_scales, wk_scales, wv_scales)
    outputs = (out_0, out_1, out_2)

    with ExitStack() as stack:
        keep = stack.enter_context(tc.tile_pool(name="keep", bufs=1))
        work = stack.enter_context(tc.tile_pool(name="work", bufs=3))
        stack.enter_context(
            tc.manual_schedule(engines={mybir.EngineType.SP, mybir.EngineType.Pool})
        )
        psum = stack.enter_context(tc.psum_pool(name="psum", bufs=8))

        table = build_rotary_table(nc, keep)
        cos = table[:, 0, :]
        rotated_sin = table[:, 1:3, :]
        identity = keep.tile([P, P], F32)
        make_identity(nc, identity[:])

        x_sb = keep.tile([P, DM], BF16, align_bytes=1024)
        nc.sync.dma_start(out=x_sb[:], in_=x.rearrange("b t k -> (b t) k"))
        rows = keep.tile([P, K_PASS], BF16)
        nc.vector.memset(rows[:], 0.0)
        nc.scalar.dma_start(out=rows[0:G, :], in_=ln_gamma.rearrange("(g c) -> g c", g=G))
        nc.scalar.dma_start(out=rows[G : 2 * G, :], in_=ln_beta.rearrange("(g c) -> g c", g=G))

        planes = keep.tile([P, 3, DM], U8, align_bytes=256)
        last_planes = keep.tile([P, 3, 2 * BANK], U8, align_bytes=256)
        nc.vector.memset(planes[:].bitcast(I32), 0)
        nc.vector.memset(last_planes[:].bitcast(I32), 0)
        spare = keep.tile([P, 13, 2, FILLER], U8)
        load_scales_on_gpsimd(nc, planes, last_planes, spare, all_scales)

        w_sb = []
        for weight in range(3):
            w_sb.append(keep.tile([P, G, DM], U32, name="w_sb%d" % weight, align_bytes=1024))
            by_quadrant = [
                scale_dmas(planes, last_planes, all_scales[weight], weight, quadrant, I32)
                for quadrant in range(4)
            ]
            small = [by_quadrant[quadrant][part] for part in range(2) for quadrant in SYNC_QUADRANTS]
            small += [dmas[2] for dmas in by_quadrant]
            for g in range(G):
                last = weight == 2 and g == G - 1
                for first, end in ((0, LAST_PART), (LAST_PART, DM)) if last else ((0, DM),):
                    nc.sync.dma_start(
                        out=w_sb[weight][:, g, first:end].bitcast(I32),
                        in_=all_words[weight][g, :, first:end, :]
                        .rearrange("q n j -> q (n j)")
                        .bitcast(I32),
                    )
                if g > 0:
                    for out, in_ in small[2 * g - 2 : 2 * g]:
                        nc.sync.dma_start(out=out, in_=in_)

        sorted_rows = keep.tile([P, PACK, P], F32)
        nc.vector.tensor_copy(out=sorted_rows[:], in_=rows[:].rearrange("r (q j) -> r j q", j=PACK))
        turned = psum.tile([P, PACK, P], F32, tag="bank")
        for j in range(PACK):
            nc.tensor.transpose(turned[:, j, :], sorted_rows[:, j, :], identity[:])
        gamma_beta = keep.tile([P, 2 * G, PACK], F32)
        nc.vector.tensor_copy(
            out=gamma_beta[:], in_=turned[:, :, 0 : 2 * G].rearrange("q j r -> q r j")
        )

        stats = keep.tile([P, G, 6], F32)
        for g in range(G):
            nc.vector.bn_stats(out=stats[:, g, :], in_=x_sb[:, K_PASS * g : K_PASS * (g + 1)])
        mean_var = keep.tile([P, 2], F32)
        nc.vector.bn_aggr(out=mean_var[:], in_=stats[:].rearrange("r g s -> r (g s)"))
        spread = keep.tile([P, 1], F32)
        nc.vector.tensor_scalar_add(out=spread[:], in0=mean_var[:, 1:2], scalar1=LN_EPS)
        nc.scalar.sqrt(out=spread[:], in_=spread[:])
        rstd = keep.tile([P, 1], F32)
        nc.vector.reciprocal(out=rstd[:], in_=spread[:])
        shift = keep.tile([P, 1], F32)
        nc.vector.scalar_tensor_tensor(
            out=shift[:], in0=mean_var[:, 0:1], scalar=-1.0, in1=rstd[:],
            op0=ALU.mult, op1=ALU.mult,
        )

        x_words = keep.tile([P, G, P], U32, align_bytes=64)
        x_scales = keep.tile([P, G, P], U8, align_bytes=64)
        for g in range(G):
            centred = work.tile([P, PACK, P], F32)
            nc.scalar.activation(
                out=centred[:],
                in_=x_sb[:, K_PASS * g : K_PASS * (g + 1)].rearrange("r (q j) -> r j q", j=PACK),
                func=ACT.Identity, scale=rstd[:, 0:1], bias=shift[:, 0:1],
            )
            transposed = psum.tile([P, PACK, P], F32, tag="bank")
            for j in range(PACK):
                nc.tensor.transpose(transposed[:, j, :], centred[:, j, :], identity[:])
            scaled = work.tile([P, P, PACK], F32)
            nc.vector.tensor_tensor(
                out=scaled[:].rearrange("q (t b) j -> q b t j", b=B),
                in0=transposed[:].rearrange("q j (b t) -> q b t j", b=B),
                in1=gamma_beta[:, g, :].unsqueeze(1).unsqueeze(1).to_broadcast([P, B, T, PACK]),
                op=ALU.mult,
            )
            xn = work.tile([P, P, PACK], BF16, align_bytes=64)
            nc.vector.tensor_tensor(
                out=xn[:], in0=scaled[:],
                in1=gamma_beta[:, G + g, :].unsqueeze(1).to_broadcast([P, P, PACK]), op=ALU.add,
            )
            nc.vector.quantize_mx(
                out=x_words[:, g, :].bitcast(FP8X4), scales=x_scales[:, g, :],
                in_=xn[:].rearrange("q r j -> q (r j)"),
            )

        banks = range(0, DM, BANK)
        for weight in range(3):
            acc = {n: psum.tile([P, BANK], F32, name="acc", tag="bank") for n in banks}
            for g in range(G):
                for n in banks:
                    if g < PLANES_PER_SLOT:
                        scale = planes[PLANE_ROWS * g : P, weight, n : n + BANK]
                    elif n < SHARED:
                        scale = last_planes[PLANE_ROWS * (n // BANK) : P, weight, 0:BANK]
                    else:
                        scale = last_planes[0:P, weight, BANK : 2 * BANK]
                    nc.tensor.matmul_mx(
                        out=acc[n][:],
                        lhsT=x_words[:, g, :].bitcast(FP8X4),
                        lhsT_scale=x_scales[:, g, :],
                        rhs=w_sb[weight][:, g, n : n + BANK].bitcast(FP8X4),
                        rhs_scale=scale,
                        start=(g == 0),
                        stop=(g == G - 1),
                    )
            whole = keep.tile([P, DM], F32, name="whole%d" % weight, align_bytes=1024)
            for turn, n in enumerate(banks):
                flat = whole[:, n : n + BANK]
                if weight == 2:
                    if turn % 2 == 0:
                        nc.scalar.copy(out=flat, in_=acc[n][:])
                    else:
                        nc.vector.tensor_copy(out=flat, in_=acc[n][:])
                    continue
                result = flat.rearrange("r (h s d) -> r h s d", s=2, d=HALF)
                u = acc[n][:].rearrange("r (h s d) -> r h s d", s=2, d=HALF)
                nc.vector.tensor_tensor(
                    out=result, in0=u,
                    in1=cos.unsqueeze(1).unsqueeze(1).to_broadcast([P, HEADS_PER_BANK, 2, HALF]),
                    op=ALU.mult,
                )
                crossed = work.tile([P, HEADS_PER_BANK, 2, HALF], F32)
                for s in range(2):
                    nc.vector.tensor_tensor(
                        out=crossed[:, :, s, :], in0=u[:, :, 1 - s, :],
                        in1=rotated_sin[:, s, :].unsqueeze(1).to_broadcast(
                            [P, HEADS_PER_BANK, HALF]
                        ),
                        op=ALU.mult,
                    )
                nc.vector.tensor_tensor(out=result, in0=result, in1=crossed[:], op=ALU.add)
            nc.sync.dma_start(out=outputs[weight].rearrange("b h t d -> t (b h) d"), in_=whole[:])
